import numpy as np
import ml_dtypes

BF16 = ml_dtypes.bfloat16


def bf(x):
    return np.asarray(x, np.float32).astype(BF16)


def f32(x):
    return np.asarray(x, np.float32)


def f64(x):
    return np.asarray(x).astype(np.float64)


def striped(idx):
    return np.tile(idx.reshape(-1, 16).T, (8, 1))


A, S, B, K, H, N = 1024, 256, 128, 4, 128, 512


def sigmoid(v):
    return 1.0 / (1.0 + np.exp(-v))


def logsig(v):
    return -np.log(1.0 + np.exp(-v))


def setup_inputs():
    return {
        "codebook": f32(np.random.random((A, S)) < 0.5),
        "z1": f32(2.0 * np.random.standard_normal((H, B))),
        "w2": bf(3.0 * np.random.standard_normal((H, H)) / np.sqrt(H)),
        "b2": f32(0.5 * np.random.standard_normal((H, 1))),
        "w3": bf(2.0 * np.random.standard_normal((H, A)) / np.sqrt(H)),
        "b3": f32(0.3 * np.random.standard_normal((A, 1))),
        "ob": f32(np.random.random((A, B)) > 0.1),
        "y": f32(np.random.random((A, B)) < 0.5),
        "offs": striped(np.concatenate([np.random.permutation(S)[:B] for _ in range(K)])),
    }


def reference(codebook, z1, w2, b2, w3, b3, ob, y, offs):
    idx = offs[:16].T.reshape(-1)
    h1 = sigmoid(f64(z1))
    h2 = sigmoid(f64(w2).T @ h1 + f64(b2))
    wc = (f64(w3).T @ h2 + f64(b3)) * f64(ob)
    neg = f64(codebook)[:, idx].reshape(A, K, B) * wc[:, None, :]
    return logsig(wc * f64(y)) + logsig(-neg).sum(axis=1)

@@ -1,0 +1,124 @@
+import concourse.mybir as mybir
+
+F32 = mybir.dt.float32
+BF16 = mybir.dt.bfloat16
+U16 = mybir.dt.uint16
+ALU = mybir.AluOpType
+FN = mybir.ActivationFunctionType
+
+P = 128
+A, S, B, K, H = 1024, 256, 128, 4, 128
+N = K * B
+BLOCKS = A // P
+TERMS = K + 1
+PIECE = B // 16
+BLOCKS_PER_BANK = 512 // B
+
+FLOPS = 2 * H * H * B + 2 * H * A * B
+
+
+def tile_mf2demo_kernel(tc, codebook, z1, w2, b2, w3, b3, ob, y, offs, out):
+    nc = tc.nc
+    with (
+        tc.tile_pool(name="held", bufs=1) as held,
+        tc.psum_pool(name="psum", bufs=1) as psum,
+    ):
+        z1_sb = held.tile([H, B], F32, name="z1_sb")
+        nc.sync.dma_start(z1_sb[:], z1)
+        offsets = held.tile([P, N // 16], U16, name="offsets")
+        nc.sync.dma_start(offsets[:], offs)
+        w2_sb = held.tile([H, H], BF16, name="w2_sb")
+        nc.scalar.dma_start(w2_sb[:], w2)
+        b2_sb = held.tile([H, 1], F32, name="b2_sb")
+        nc.scalar.dma_start(b2_sb[:], b2)
+        w3_sb = held.tile([H, A], BF16, name="w3_sb")
+        nc.scalar.dma_start(w3_sb[:], w3)
+        b3_sb = held.tile([P, BLOCKS], F32, name="b3_sb")
+        with nc.allow_non_contiguous_dma(reason="b3 goes one element to a partition"):
+            nc.scalar.dma_start(b3_sb[:], b3.rearrange("(i p) o -> p (i o)", p=P))
+
+        windows = [held.tile([P, S], F32, name=f"window{i}") for i in range(BLOCKS)]
+        ob_sb = held.tile([P, BLOCKS, B], F32, name="ob_sb")
+        y_sb = held.tile([P, BLOCKS, B], F32, name="y_sb")
+        for i in range(BLOCKS):
+            rows = slice(i * P, (i + 1) * P)
+            nc.sync.dma_start(ob_sb[:, i, :], ob[rows, :])
+            nc.sync.dma_start(windows[i][:], codebook[rows, :])
+            nc.scalar.dma_start(y_sb[:, i, :], y[rows, :])
+
+        h1 = held.tile([H, B], BF16, name="h1")
+        nc.scalar.activation(h1[:], z1_sb[:], FN.Sigmoid)
+        ps_h2 = psum.tile([H, B], F32, name="ps_h2")
+        nc.tensor.matmul(ps_h2[:], lhsT=w2_sb[:], rhs=h1[:], start=True, stop=True)
+        h2 = held.tile([H, B], BF16, name="h2")
+        nc.scalar.activation(h2[:], ps_h2[:], FN.Sigmoid, bias=b2_sb[:, 0:1])
+        ps_wc = [
+            psum.tile([P, BLOCKS_PER_BANK, B], F32, name=f"ps_wc{j}")
+            for j in range(BLOCKS // BLOCKS_PER_BANK)
+        ]
+        for i in range(BLOCKS):
+            nc.tensor.matmul(
+                ps_wc[i // BLOCKS_PER_BANK][:, i % BLOCKS_PER_BANK, :],
+                lhsT=w3_sb[:, i * P : (i + 1) * P],
+                rhs=h2[:],
+                start=True,
+                stop=True,
+            )
+
+        wc = held.tile([P, BLOCKS, B], F32, name="wc")
+        t = held.tile([P, BLOCKS, TERMS, B], F32, name="t")
+        mag = held.tile([P, BLOCKS, TERMS, B], F32, name="mag")
+        sig = held.tile([P, BLOCKS, TERMS, B], F32, name="sig")
+        for i in range(BLOCKS):
+            nc.vector.scalar_tensor_tensor(
+                out=wc[:, i, :],
+                in0=ps_wc[i // BLOCKS_PER_BANK][:, i % BLOCKS_PER_BANK, :],
+                scalar=b3_sb[:, i : i + 1],
+                in1=ob_sb[:, i, :],
+                op0=ALU.add,
+                op1=ALU.mult,
+            )
+            for k in range(K):
+                nc.vector.tensor_tensor(
+                    t[:, i, k, :],
+                    windows[i][:].indirect(offsets[:, k * PIECE : (k + 1) * PIECE]),
+                    wc[:, i, :],
+                    ALU.mult,
+                )
+            nc.vector.scalar_tensor_tensor(
+                out=t[:, i, K, :],
+                in0=wc[:, i, :],
+                scalar=-1.0,
+                in1=y_sb[:, i, :],
+                op0=ALU.mult,
+                op1=ALU.mult,
+            )
+            nc.scalar.activation(mag[:, i], t[:, i], FN.Abs)
+            nc.scalar.activation(sig[:, i], mag[:, i], FN.Sigmoid)
+
+        ramp = held.tile([P, BLOCKS, B], F32, name="ramp")
+        for i in range(BLOCKS):
+            nc.vector.tensor_scalar_max(ramp[:, i, :], t[:, i, 0, :], 0.0)
+            for k in range(1, TERMS):
+                nc.vector.scalar_tensor_tensor(
+                    out=ramp[:, i, :],
+                    in0=t[:, i, k, :],
+                    scalar=0.0,
+                    in1=ramp[:, i, :],
+                    op0=ALU.max,
+                    op1=ALU.add,
+                )
+
+        prod = held.tile([P, BLOCKS, B], F32, name="prod")
+        lnprod = held.tile([P, BLOCKS, B], F32, name="lnprod")
+        result = held.tile([P, BLOCKS, B], F32, name="result")
+        for i in range(BLOCKS + 1):
+            if i < BLOCKS:
+                nc.vector.tensor_tensor(prod[:, i, :], sig[:, i, 0, :], sig[:, i, 1, :], ALU.mult)
+                for k in range(2, TERMS):
+                    nc.vector.tensor_tensor(prod[:, i, :], prod[:, i, :], sig[:, i, k, :], ALU.mult)
+                nc.scalar.activation(lnprod[:, i, :], prod[:, i, :], FN.Ln)
+            if i > 0:
+                j = i - 1
+                nc.vector.tensor_tensor(result[:, j, :], lnprod[:, j, :], ramp[:, j, :], ALU.subtract)
+                nc.sync.dma_start(out[j * P : (j + 1) * P, :], result[:, j, :])

@@ -13,6 +13,7 @@ BLOCKS = A // P
 TERMS = K + 1
 PIECE = B // 16
 BLOCKS_PER_BANK = 512 // B
+LOAD_BLOCKS = 4
 
 FLOPS = 2 * H * H * B + 2 * H * A * B
 
@@ -25,26 +26,30 @@ def tile_mf2demo_kernel(tc, codebook, z1, w2, b2, w3, b3, ob, y, offs, out):
     ):
         z1_sb = held.tile([H, B], F32, name="z1_sb")
         nc.sync.dma_start(z1_sb[:], z1)
-        offsets = held.tile([P, N // 16], U16, name="offsets")
-        nc.sync.dma_start(offsets[:], offs)
         w2_sb = held.tile([H, H], BF16, name="w2_sb")
-        nc.scalar.dma_start(w2_sb[:], w2)
+        nc.sync.dma_start(w2_sb[:], w2)
         b2_sb = held.tile([H, 1], F32, name="b2_sb")
-        nc.scalar.dma_start(b2_sb[:], b2)
+        nc.sync.dma_start(b2_sb[:], b2)
         w3_sb = held.tile([H, A], BF16, name="w3_sb")
-        nc.scalar.dma_start(w3_sb[:], w3)
+        nc.sync.dma_start(w3_sb[:], w3)
         b3_sb = held.tile([P, BLOCKS], F32, name="b3_sb")
         with nc.allow_non_contiguous_dma(reason="b3 goes one element to a partition"):
-            nc.scalar.dma_start(b3_sb[:], b3.rearrange("(i p) o -> p (i o)", p=P))
+            nc.sync.dma_start(b3_sb[:], b3.rearrange("(i p) o -> p (i o)", p=P))
+        offsets = held.tile([P, N // 16], U16, name="offsets")
+        nc.sync.dma_start(offsets[:], offs)
 
         windows = [held.tile([P, S], F32, name=f"window{i}") for i in range(BLOCKS)]
         ob_sb = held.tile([P, BLOCKS, B], F32, name="ob_sb")
         y_sb = held.tile([P, BLOCKS, B], F32, name="y_sb")
-        for i in range(BLOCKS):
-            rows = slice(i * P, (i + 1) * P)
-            nc.sync.dma_start(ob_sb[:, i, :], ob[rows, :])
-            nc.sync.dma_start(windows[i][:], codebook[rows, :])
-            nc.scalar.dma_start(y_sb[:, i, :], y[rows, :])
+        ob_blocks = ob.rearrange("(i p) u -> p i u", p=P)
+        y_blocks = y.rearrange("(i p) u -> p i u", p=P)
+        for first in range(0, BLOCKS, LOAD_BLOCKS):
+            group = slice(first, first + LOAD_BLOCKS)
+            nc.sync.dma_start(ob_sb[:, group, :], ob_blocks[:, group, :])
+            nc.sync.dma_start(windows[first][:], codebook[first * P : (first + 1) * P, :])
+            nc.sync.dma_start(y_sb[:, group, :], y_blocks[:, group, :])
+            for i in range(first + 1, first + LOAD_BLOCKS):
+                nc.sync.dma_start(windows[i][:], codebook[i * P : (i + 1) * P, :])
 
         h1 = held.tile([H, B], BF16, name="h1")
         nc.scalar.activation(h1[:], z1_sb[:], FN.Sigmoid)

@@ -74,6 +74,7 @@ def tile_mf2demo_kernel(tc, codebook, z1, w2, b2, w3, b3, ob, y, offs, out):
         t = held.tile([P, BLOCKS, TERMS, B], F32, name="t")
         mag = held.tile([P, BLOCKS, TERMS, B], F32, name="mag")
         sig = held.tile([P, BLOCKS, TERMS, B], F32, name="sig")
+        prod = held.tile([P, BLOCKS, B], F32, name="prod")
         for i in range(BLOCKS):
             nc.vector.scalar_tensor_tensor(
                 out=wc[:, i, :],
@@ -100,6 +101,9 @@ def tile_mf2demo_kernel(tc, codebook, z1, w2, b2, w3, b3, ob, y, offs, out):
             )
             nc.scalar.activation(mag[:, i], t[:, i], FN.Abs)
             nc.scalar.activation(sig[:, i], mag[:, i], FN.Sigmoid)
+            nc.gpsimd.tensor_tensor(prod[:, i, :], sig[:, i, 0, :], sig[:, i, 1, :], ALU.mult)
+            for k in range(2, TERMS):
+                nc.gpsimd.tensor_tensor(prod[:, i, :], prod[:, i, :], sig[:, i, k, :], ALU.mult)
 
         ramp = held.tile([P, BLOCKS, B], F32, name="ramp")
         for i in range(BLOCKS):
@@ -114,16 +118,9 @@ def tile_mf2demo_kernel(tc, codebook, z1, w2, b2, w3, b3, ob, y, offs, out):
                     op1=ALU.add,
                 )
 
-        prod = held.tile([P, BLOCKS, B], F32, name="prod")
         lnprod = held.tile([P, BLOCKS, B], F32, name="lnprod")
         result = held.tile([P, BLOCKS, B], F32, name="result")
-        for i in range(BLOCKS + 1):
-            if i < BLOCKS:
-                nc.vector.tensor_tensor(prod[:, i, :], sig[:, i, 0, :], sig[:, i, 1, :], ALU.mult)
-                for k in range(2, TERMS):
-                    nc.vector.tensor_tensor(prod[:, i, :], prod[:, i, :], sig[:, i, k, :], ALU.mult)
-                nc.scalar.activation(lnprod[:, i, :], prod[:, i, :], FN.Ln)
-            if i > 0:
-                j = i - 1
-                nc.vector.tensor_tensor(result[:, j, :], lnprod[:, j, :], ramp[:, j, :], ALU.subtract)
-                nc.sync.dma_start(out[j * P : (j + 1) * P, :], result[:, j, :])
+        for i in range(BLOCKS):
+            nc.scalar.activation(lnprod[:, i, :], prod[:, i, :], FN.Ln)
+            nc.vector.tensor_tensor(result[:, i, :], lnprod[:, i, :], ramp[:, i, :], ALU.subtract)
+            nc.sync.dma_start(out[i * P : (i + 1) * P, :], result[:, i, :])

@@ -1,4 +1,5 @@
 import concourse.mybir as mybir
+from concourse.masks import make_identity
 
 F32 = mybir.dt.float32
 BF16 = mybir.dt.bfloat16
@@ -14,6 +15,7 @@ TERMS = K + 1
 PIECE = B // 16
 BLOCKS_PER_BANK = 512 // B
 LOAD_BLOCKS = 4
+SCALAR_RELU_BLOCKS = 4
 
 FLOPS = 2 * H * H * B + 2 * H * A * B
 
@@ -51,6 +53,9 @@ def tile_mf2demo_kernel(tc, codebook, z1, w2, b2, w3, b3, ob, y, offs, out):
             for i in range(first + 1, first + LOAD_BLOCKS):
                 nc.sync.dma_start(windows[i][:], codebook[i * P : (i + 1) * P, :])
 
+        identity = held.tile([P, P], F32, name="identity")
+        make_identity(nc, identity[:])
+
         h1 = held.tile([H, B], BF16, name="h1")
         nc.scalar.activation(h1[:], z1_sb[:], FN.Sigmoid)
         ps_h2 = psum.tile([H, B], F32, name="ps_h2")
@@ -61,6 +66,16 @@ def tile_mf2demo_kernel(tc, codebook, z1, w2, b2, w3, b3, ob, y, offs, out):
             psum.tile([P, BLOCKS_PER_BANK, B], F32, name=f"ps_wc{j}")
             for j in range(BLOCKS // BLOCKS_PER_BANK)
         ]
+
+        wc = held.tile([P, BLOCKS, B], F32, name="wc")
+        t = held.tile([P, BLOCKS, TERMS, B], F32, name="t")
+        mag = held.tile([P, BLOCKS, TERMS, B], F32, name="mag")
+        sig = held.tile([P, BLOCKS, TERMS, B], F32, name="sig")
+        pos = held.tile([P, BLOCKS, TERMS, B], F32, name="pos")
+        ps_ramp = [
+            psum.tile([P, BLOCKS_PER_BANK, B], F32, name=f"ps_ramp{j}")
+            for j in range(BLOCKS // BLOCKS_PER_BANK)
+        ]
         for i in range(BLOCKS):
             nc.tensor.matmul(
                 ps_wc[i // BLOCKS_PER_BANK][:, i % BLOCKS_PER_BANK, :],
@@ -69,13 +84,6 @@ def tile_mf2demo_kernel(tc, codebook, z1, w2, b2, w3, b3, ob, y, offs, out):
                 start=True,
                 stop=True,
             )
-
-        wc = held.tile([P, BLOCKS, B], F32, name="wc")
-        t = held.tile([P, BLOCKS, TERMS, B], F32, name="t")
-        mag = held.tile([P, BLOCKS, TERMS, B], F32, name="mag")
-        sig = held.tile([P, BLOCKS, TERMS, B], F32, name="sig")
-        prod = held.tile([P, BLOCKS, B], F32, name="prod")
-        for i in range(BLOCKS):
             nc.vector.scalar_tensor_tensor(
                 out=wc[:, i, :],
                 in0=ps_wc[i // BLOCKS_PER_BANK][:, i % BLOCKS_PER_BANK, :],
@@ -101,26 +109,37 @@ def tile_mf2demo_kernel(tc, codebook, z1, w2, b2, w3, b3, ob, y, offs, out):
             )
             nc.scalar.activation(mag[:, i], t[:, i], FN.Abs)
             nc.scalar.activation(sig[:, i], mag[:, i], FN.Sigmoid)
-            nc.gpsimd.tensor_tensor(prod[:, i, :], sig[:, i, 0, :], sig[:, i, 1, :], ALU.mult)
-            for k in range(2, TERMS):
-                nc.gpsimd.tensor_tensor(prod[:, i, :], prod[:, i, :], sig[:, i, k, :], ALU.mult)
+            if i < SCALAR_RELU_BLOCKS:
+                nc.scalar.activation(pos[:, i], t[:, i], FN.Relu)
 
-        ramp = held.tile([P, BLOCKS, B], F32, name="ramp")
+        for i in range(SCALAR_RELU_BLOCKS, BLOCKS):
+            nc.vector.tensor_scalar_max(pos[:, i], t[:, i], 0.0)
+
         for i in range(BLOCKS):
-            nc.vector.tensor_scalar_max(ramp[:, i, :], t[:, i, 0, :], 0.0)
-            for k in range(1, TERMS):
-                nc.vector.scalar_tensor_tensor(
-                    out=ramp[:, i, :],
-                    in0=t[:, i, k, :],
-                    scalar=0.0,
-                    in1=ramp[:, i, :],
-                    op0=ALU.max,
-                    op1=ALU.add,
+            for k in range(TERMS):
+                nc.tensor.matmul(
+                    ps_ramp[i // BLOCKS_PER_BANK][:, i % BLOCKS_PER_BANK, :],
+                    lhsT=identity[:],
+                    rhs=pos[:, i, k, :],
+                    start=(k == 0),
+                    stop=(k == TERMS - 1),
                 )
 
+        prod = held.tile([P, BLOCKS, B], F32, name="prod")
         lnprod = held.tile([P, BLOCKS, B], F32, name="lnprod")
         result = held.tile([P, BLOCKS, B], F32, name="result")
-        for i in range(BLOCKS):
-            nc.scalar.activation(lnprod[:, i, :], prod[:, i, :], FN.Ln)
-            nc.vector.tensor_tensor(result[:, i, :], lnprod[:, i, :], ramp[:, i, :], ALU.subtract)
-            nc.sync.dma_start(out[i * P : (i + 1) * P, :], result[:, i, :])
+        for i in range(BLOCKS + 1):
+            if i < BLOCKS:
+                nc.vector.tensor_tensor(prod[:, i, :], sig[:, i, 0, :], sig[:, i, 1, :], ALU.mult)
+                for k in range(2, TERMS):
+                    nc.vector.tensor_tensor(prod[:, i, :], prod[:, i, :], sig[:, i, k, :], ALU.mult)
+                nc.scalar.activation(lnprod[:, i, :], prod[:, i, :], FN.Ln)
+            if i > 0:
+                j = i - 1
+                nc.vector.tensor_tensor(
+                    result[:, j, :],
+                    lnprod[:, j, :],
+                    ps_ramp[j // BLOCKS_PER_BANK][:, j % BLOCKS_PER_BANK, :],
+                    ALU.subtract,
+                )
+                nc.sync.dma_start(out[j * P : (j + 1) * P, :], result[:, j, :])

@@ -13,9 +13,9 @@ N = K * B
 BLOCKS = A // P
 TERMS = K + 1
 PIECE = B // 16
-BLOCKS_PER_BANK = 512 // B
-LOAD_BLOCKS = 4
-SCALAR_RELU_BLOCKS = 4
+BANK = 512 // B
+BANKS = BLOCKS // BANK
+SCALAR_RELU_BLOCKS = 5
 
 FLOPS = 2 * H * H * B + 2 * H * A * B
 
@@ -45,12 +45,13 @@ def tile_mf2demo_kernel(tc, codebook, z1, w2, b2, w3, b3, ob, y, offs, out):
         y_sb = held.tile([P, BLOCKS, B], F32, name="y_sb")
         ob_blocks = ob.rearrange("(i p) u -> p i u", p=P)
         y_blocks = y.rearrange("(i p) u -> p i u", p=P)
-        for first in range(0, BLOCKS, LOAD_BLOCKS):
-            group = slice(first, first + LOAD_BLOCKS)
+        out_blocks = out.rearrange("(i p) u -> p i u", p=P)
+        for first in range(0, BLOCKS, BANK):
+            group = slice(first, first + BANK)
             nc.sync.dma_start(ob_sb[:, group, :], ob_blocks[:, group, :])
             nc.sync.dma_start(windows[first][:], codebook[first * P : (first + 1) * P, :])
             nc.sync.dma_start(y_sb[:, group, :], y_blocks[:, group, :])
-            for i in range(first + 1, first + LOAD_BLOCKS):
+            for i in range(first + 1, first + BANK):
                 nc.sync.dma_start(windows[i][:], codebook[i * P : (i + 1) * P, :])
 
         identity = held.tile([P, P], F32, name="identity")
@@ -62,36 +63,27 @@ def tile_mf2demo_kernel(tc, codebook, z1, w2, b2, w3, b3, ob, y, offs, out):
         nc.tensor.matmul(ps_h2[:], lhsT=w2_sb[:], rhs=h1[:], start=True, stop=True)
         h2 = held.tile([H, B], BF16, name="h2")
         nc.scalar.activation(h2[:], ps_h2[:], FN.Sigmoid, bias=b2_sb[:, 0:1])
-        ps_wc = [
-            psum.tile([P, BLOCKS_PER_BANK, B], F32, name=f"ps_wc{j}")
-            for j in range(BLOCKS // BLOCKS_PER_BANK)
-        ]
 
+        ps_wc = [psum.tile([P, BANK, B], F32, name=f"ps_wc{g}") for g in range(BANKS)]
+        ps_ramp = [psum.tile([P, BANK, B], F32, name=f"ps_ramp{g}") for g in range(BANKS)]
+        biased = held.tile([P, BLOCKS, B], F32, name="biased")
         wc = held.tile([P, BLOCKS, B], F32, name="wc")
         t = held.tile([P, BLOCKS, TERMS, B], F32, name="t")
+        pos = held.tile([P, BLOCKS, TERMS, B], F32, name="pos")
         mag = held.tile([P, BLOCKS, TERMS, B], F32, name="mag")
         sig = held.tile([P, BLOCKS, TERMS, B], F32, name="sig")
-        pos = held.tile([P, BLOCKS, TERMS, B], F32, name="pos")
-        ps_ramp = [
-            psum.tile([P, BLOCKS_PER_BANK, B], F32, name=f"ps_ramp{j}")
-            for j in range(BLOCKS // BLOCKS_PER_BANK)
-        ]
         for i in range(BLOCKS):
             nc.tensor.matmul(
-                ps_wc[i // BLOCKS_PER_BANK][:, i % BLOCKS_PER_BANK, :],
+                ps_wc[i // BANK][:, i % BANK, :],
                 lhsT=w3_sb[:, i * P : (i + 1) * P],
                 rhs=h2[:],
                 start=True,
                 stop=True,
             )
-            nc.vector.scalar_tensor_tensor(
-                out=wc[:, i, :],
-                in0=ps_wc[i // BLOCKS_PER_BANK][:, i % BLOCKS_PER_BANK, :],
-                scalar=b3_sb[:, i : i + 1],
-                in1=ob_sb[:, i, :],
-                op0=ALU.add,
-                op1=ALU.mult,
+            nc.scalar.activation(
+                biased[:, i, :], ps_wc[i // BANK][:, i % BANK, :], FN.Identity, bias=b3_sb[:, i : i + 1]
             )
+            nc.vector.tensor_tensor(wc[:, i, :], biased[:, i, :], ob_sb[:, i, :], ALU.mult)
             for k in range(K):
                 nc.vector.tensor_tensor(
                     t[:, i, k, :],
@@ -107,10 +99,12 @@ def tile_mf2demo_kernel(tc, codebook, z1, w2, b2, w3, b3, ob, y, offs, out):
                 op0=ALU.mult,
                 op1=ALU.mult,
             )
-            nc.scalar.activation(mag[:, i], t[:, i], FN.Abs)
-            nc.scalar.activation(sig[:, i], mag[:, i], FN.Sigmoid)
             if i < SCALAR_RELU_BLOCKS:
                 nc.scalar.activation(pos[:, i], t[:, i], FN.Relu)
+            nc.scalar.activation(mag[:, i], t[:, i], FN.Abs)
+            nc.scalar.activation(sig[:, i, 0:K, :], mag[:, i, 0:K, :], FN.Sigmoid)
+
+        nc.scalar.activation(sig[:, :, K, :], mag[:, :, K, :], FN.Sigmoid)
 
         for i in range(SCALAR_RELU_BLOCKS, BLOCKS):
             nc.vector.tensor_scalar_max(pos[:, i], t[:, i], 0.0)
@@ -118,7 +112,7 @@ def tile_mf2demo_kernel(tc, codebook, z1, w2, b2, w3, b3, ob, y, offs, out):
         for i in range(BLOCKS):
             for k in range(TERMS):
                 nc.tensor.matmul(
-                    ps_ramp[i // BLOCKS_PER_BANK][:, i % BLOCKS_PER_BANK, :],
+                    ps_ramp[i // BANK][:, i % BANK, :],
                     lhsT=identity[:],
                     rhs=pos[:, i, k, :],
                     start=(k == 0),
@@ -128,18 +122,11 @@ def tile_mf2demo_kernel(tc, codebook, z1, w2, b2, w3, b3, ob, y, offs, out):
         prod = held.tile([P, BLOCKS, B], F32, name="prod")
         lnprod = held.tile([P, BLOCKS, B], F32, name="lnprod")
         result = held.tile([P, BLOCKS, B], F32, name="result")
-        for i in range(BLOCKS + 1):
-            if i < BLOCKS:
-                nc.vector.tensor_tensor(prod[:, i, :], sig[:, i, 0, :], sig[:, i, 1, :], ALU.mult)
-                for k in range(2, TERMS):
-                    nc.vector.tensor_tensor(prod[:, i, :], prod[:, i, :], sig[:, i, k, :], ALU.mult)
-                nc.scalar.activation(lnprod[:, i, :], prod[:, i, :], FN.Ln)
-            if i > 0:
-                j = i - 1
-                nc.vector.tensor_tensor(
-                    result[:, j, :],
-                    lnprod[:, j, :],
-                    ps_ramp[j // BLOCKS_PER_BANK][:, j % BLOCKS_PER_BANK, :],
-                    ALU.subtract,
-                )
-                nc.sync.dma_start(out[j * P : (j + 1) * P, :], result[:, j, :])
+        for g in range(BANKS):
+            group = slice(g * BANK, (g + 1) * BANK)
+            nc.vector.tensor_tensor(prod[:, group, :], sig[:, group, 0, :], sig[:, group, 1, :], ALU.mult)
+            for k in range(2, TERMS):
+                nc.vector.tensor_tensor(prod[:, group, :], prod[:, group, :], sig[:, group, k, :], ALU.mult)
+            nc.scalar.activation(lnprod[:, group, :], prod[:, group, :], FN.Ln)
+            nc.vector.tensor_tensor(result[:, group, :], lnprod[:, group, :], ps_ramp[g][:], ALU.subtract)
+            nc.sync.dma_start(out_blocks[:, group, :], result[:, group, :])

@@ -34,9 +34,9 @@ def tile_mf2demo_kernel(tc, codebook, z1, w2, b2, w3, b3, ob, y, offs, out):
         nc.sync.dma_start(b2_sb[:], b2)
         w3_sb = held.tile([H, A], BF16, name="w3_sb")
         nc.sync.dma_start(w3_sb[:], w3)
-        b3_sb = held.tile([P, BLOCKS], F32, name="b3_sb")
-        with nc.allow_non_contiguous_dma(reason="b3 goes one element to a partition"):
-            nc.sync.dma_start(b3_sb[:], b3.rearrange("(i p) o -> p (i o)", p=P))
+        b3_rows = held.tile([P, P], F32, name="b3_rows")
+        nc.vector.memset(b3_rows[:], 0.0)
+        nc.sync.dma_start(b3_rows[0:BLOCKS, :], b3.rearrange("(i p) o -> i (p o)", p=P))
         offsets = held.tile([P, N // 16], U16, name="offsets")
         nc.sync.dma_start(offsets[:], offs)
 
@@ -63,6 +63,11 @@ def tile_mf2demo_kernel(tc, codebook, z1, w2, b2, w3, b3, ob, y, offs, out):
         nc.tensor.matmul(ps_h2[:], lhsT=w2_sb[:], rhs=h1[:], start=True, stop=True)
         h2 = held.tile([H, B], BF16, name="h2")
         nc.scalar.activation(h2[:], ps_h2[:], FN.Sigmoid, bias=b2_sb[:, 0:1])
+
+        ps_b3 = psum.tile([P, P], F32, name="ps_b3")
+        nc.tensor.transpose(ps_b3[:], b3_rows[:], identity[:])
+        b3_sb = held.tile([P, BLOCKS], F32, name="b3_sb")
+        nc.vector.tensor_copy(b3_sb[:], ps_b3[:, 0:BLOCKS])
 
         ps_wc = [psum.tile([P, BANK, B], F32, name=f"ps_wc{g}") for g in range(BANKS)]
         ps_ramp = [psum.tile([P, BANK, B], F32, name=f"ps_ramp{g}") for g in range(BANKS)]

@@ -15,6 +15,7 @@ TERMS = K + 1
 PIECE = B // 16
 BANK = 512 // B
 BANKS = BLOCKS // BANK
+QUAD = 32
 SCALAR_RELU_BLOCKS = 5
 
 FLOPS = 2 * H * H * B + 2 * H * A * B
@@ -30,13 +31,17 @@ def tile_mf2demo_kernel(tc, codebook, z1, w2, b2, w3, b3, ob, y, offs, out):
         nc.sync.dma_start(z1_sb[:], z1)
         w2_sb = held.tile([H, H], BF16, name="w2_sb")
         nc.sync.dma_start(w2_sb[:], w2)
-        b2_sb = held.tile([H, 1], F32, name="b2_sb")
-        nc.sync.dma_start(b2_sb[:], b2)
+        bias_rows = held.tile([P, QUAD], F32, name="bias_rows", align_bytes=64)
+        bias_cols = held.tile([P, QUAD], F32, name="bias_cols", align_bytes=64)
+        nc.vector.memset(bias_rows[:], 0.0)
+        rows_by_quadrant = bias_rows[:].rearrange("(c r) e -> c r e", r=QUAD)
+        nc.sync.dma_start(rows_by_quadrant[:, BLOCKS, :], b2.rearrange("(c e) o -> c (e o)", e=QUAD))
+        b3_by_quadrant = b3.rearrange("(i c e) o -> c i (e o)", i=BLOCKS, e=QUAD)
+        for c in range(P // QUAD):
+            nc.sync.dma_start(bias_rows[c * QUAD : c * QUAD + BLOCKS, :], b3_by_quadrant[c])
+        nc.vector.transpose(bias_cols[:], bias_rows[:])
         w3_sb = held.tile([H, A], BF16, name="w3_sb")
         nc.sync.dma_start(w3_sb[:], w3)
-        b3_rows = held.tile([P, P], F32, name="b3_rows")
-        nc.vector.memset(b3_rows[:], 0.0)
-        nc.sync.dma_start(b3_rows[0:BLOCKS, :], b3.rearrange("(i p) o -> i (p o)", p=P))
         offsets = held.tile([P, N // 16], U16, name="offsets")
         nc.sync.dma_start(offsets[:], offs)
 
@@ -62,12 +67,7 @@ def tile_mf2demo_kernel(tc, codebook, z1, w2, b2, w3, b3, ob, y, offs, out):
         ps_h2 = psum.tile([H, B], F32, name="ps_h2")
         nc.tensor.matmul(ps_h2[:], lhsT=w2_sb[:], rhs=h1[:], start=True, stop=True)
         h2 = held.tile([H, B], BF16, name="h2")
-        nc.scalar.activation(h2[:], ps_h2[:], FN.Sigmoid, bias=b2_sb[:, 0:1])
-
-        ps_b3 = psum.tile([P, P], F32, name="ps_b3")
-        nc.tensor.transpose(ps_b3[:], b3_rows[:], identity[:])
-        b3_sb = held.tile([P, BLOCKS], F32, name="b3_sb")
-        nc.vector.tensor_copy(b3_sb[:], ps_b3[:, 0:BLOCKS])
+        nc.scalar.activation(h2[:], ps_h2[:], FN.Sigmoid, bias=bias_cols[:, BLOCKS : BLOCKS + 1])
 
         ps_wc = [psum.tile([P, BANK, B], F32, name=f"ps_wc{g}") for g in range(BANKS)]
         ps_ramp = [psum.tile([P, BANK, B], F32, name=f"ps_ramp{g}") for g in range(BANKS)]
@@ -78,16 +78,11 @@ def tile_mf2demo_kernel(tc, codebook, z1, w2, b2, w3, b3, ob, y, offs, out):
         mag = held.tile([P, BLOCKS, TERMS, B], F32, name="mag")
         sig = held.tile([P, BLOCKS, TERMS, B], F32, name="sig")
         for i in range(BLOCKS):
-            nc.tensor.matmul(
-                ps_wc[i // BANK][:, i % BANK, :],
-                lhsT=w3_sb[:, i * P : (i + 1) * P],
-                rhs=h2[:],
-                start=True,
-                stop=True,
-            )
-            nc.scalar.activation(
-                biased[:, i, :], ps_wc[i // BANK][:, i % BANK, :], FN.Identity, bias=b3_sb[:, i : i + 1]
-            )
+            ps_block = ps_wc[i % BANKS][:, i // BANKS, :]
+            nc.tensor.matmul(ps_block, lhsT=w3_sb[:, i * P : (i + 1) * P], rhs=h2[:], start=True, stop=True)
+            nc.scalar.activation(biased[:, i, :], ps_block, FN.Identity, bias=bias_cols[:, i : i + 1])
+
+        for i in range(BLOCKS):
             nc.vector.tensor_tensor(wc[:, i, :], biased[:, i, :], ob_sb[:, i, :], ALU.mult)
             for k in range(K):
                 nc.vector.tensor_tensor(

@@ -1,3 +1,5 @@
+import math
+
 import concourse.mybir as mybir
 from concourse.masks import make_identity
 
@@ -16,10 +18,11 @@ PIECE = B // 16
 BANK = 512 // B
 BANKS = BLOCKS // BANK
 QUAD = 32
-SCALAR_RELU_BLOCKS = 5
+PAIR = 2
+PAIRS = BLOCKS // PAIR
+LAG = 2
 
 FLOPS = 2 * H * H * B + 2 * H * A * B
-
 
 def tile_mf2demo_kernel(tc, codebook, z1, w2, b2, w3, b3, ob, y, offs, out):
     nc = tc.nc
@@ -51,16 +54,21 @@ def tile_mf2demo_kernel(tc, codebook, z1, w2, b2, w3, b3, ob, y, offs, out):
         ob_blocks = ob.rearrange("(i p) u -> p i u", p=P)
         y_blocks = y.rearrange("(i p) u -> p i u", p=P)
         out_blocks = out.rearrange("(i p) u -> p i u", p=P)
-        for first in range(0, BLOCKS, BANK):
-            group = slice(first, first + BANK)
-            nc.sync.dma_start(ob_sb[:, group, :], ob_blocks[:, group, :])
-            nc.sync.dma_start(windows[first][:], codebook[first * P : (first + 1) * P, :])
-            nc.sync.dma_start(y_sb[:, group, :], y_blocks[:, group, :])
-            for i in range(first + 1, first + BANK):
+        halves = [slice(first, first + BANK) for first in range(0, BLOCKS, BANK)]
+        nc.sync.dma_start(ob_sb[:, halves[0], :], ob_blocks[:, halves[0], :])
+        nc.sync.dma_start(windows[0][:], codebook[0:P, :])
+        nc.sync.dma_start(ob_sb[:, halves[1], :], ob_blocks[:, halves[1], :])
+        for half in halves:
+            nc.sync.dma_start(y_sb[:, half, :], y_blocks[:, half, :])
+            for i in range(max(half.start, 1), half.stop):
                 nc.sync.dma_start(windows[i][:], codebook[i * P : (i + 1) * P, :])
 
         identity = held.tile([P, P], F32, name="identity")
         make_identity(nc, identity[:])
+        minus_identity = held.tile([P, P], F32, name="minus_identity")
+        nc.vector.tensor_scalar_mul(minus_identity[:], identity[:], -1.0)
+        identity_bf = held.tile([P, P], BF16, name="identity_bf")
+        nc.vector.tensor_copy(identity_bf[:], identity[:])
 
         h1 = held.tile([H, B], BF16, name="h1")
         nc.scalar.activation(h1[:], z1_sb[:], FN.Sigmoid)
@@ -70,20 +78,24 @@ def tile_mf2demo_kernel(tc, codebook, z1, w2, b2, w3, b3, ob, y, offs, out):
         nc.scalar.activation(h2[:], ps_h2[:], FN.Sigmoid, bias=bias_cols[:, BLOCKS : BLOCKS + 1])
 
         ps_wc = [psum.tile([P, BANK, B], F32, name=f"ps_wc{g}") for g in range(BANKS)]
-        ps_ramp = [psum.tile([P, BANK, B], F32, name=f"ps_ramp{g}") for g in range(BANKS)]
         biased = held.tile([P, BLOCKS, B], F32, name="biased")
         wc = held.tile([P, BLOCKS, B], F32, name="wc")
-        t = held.tile([P, BLOCKS, TERMS, B], F32, name="t")
-        pos = held.tile([P, BLOCKS, TERMS, B], F32, name="pos")
-        mag = held.tile([P, BLOCKS, TERMS, B], F32, name="mag")
-        sig = held.tile([P, BLOCKS, TERMS, B], F32, name="sig")
         for i in range(BLOCKS):
             ps_block = ps_wc[i % BANKS][:, i // BANKS, :]
             nc.tensor.matmul(ps_block, lhsT=w3_sb[:, i * P : (i + 1) * P], rhs=h2[:], start=True, stop=True)
             nc.scalar.activation(biased[:, i, :], ps_block, FN.Identity, bias=bias_cols[:, i : i + 1])
 
-        for i in range(BLOCKS):
+        t = held.tile([P, BLOCKS, TERMS, B], F32, name="t")
+        sgn = held.tile([P, BLOCKS, TERMS, B], BF16, name="sgn")
+        ps_count = [psum.tile([P, PAIR, B], F32, name=f"ps_count{j}") for j in range(PAIRS)]
+        absq = held.tile([P, BLOCKS, B], F32, name="absq")
+        loss = held.tile([P, BLOCKS, B], F32, name="loss")
+        result = held.tile([P, BLOCKS, B], F32, name="result")
+
+        def mask(i):
             nc.vector.tensor_tensor(wc[:, i, :], biased[:, i, :], ob_sb[:, i, :], ALU.mult)
+
+        def look_up(i):
             for k in range(K):
                 nc.vector.tensor_tensor(
                     t[:, i, k, :],
@@ -91,42 +103,54 @@ def tile_mf2demo_kernel(tc, codebook, z1, w2, b2, w3, b3, ob, y, offs, out):
                     wc[:, i, :],
                     ALU.mult,
                 )
-            nc.vector.scalar_tensor_tensor(
-                out=t[:, i, K, :],
-                in0=wc[:, i, :],
-                scalar=-1.0,
-                in1=y_sb[:, i, :],
-                op0=ALU.mult,
-                op1=ALU.mult,
-            )
-            if i < SCALAR_RELU_BLOCKS:
-                nc.scalar.activation(pos[:, i], t[:, i], FN.Relu)
-            nc.scalar.activation(mag[:, i], t[:, i], FN.Abs)
-            nc.scalar.activation(sig[:, i, 0:K, :], mag[:, i, 0:K, :], FN.Sigmoid)
-
-        nc.scalar.activation(sig[:, :, K, :], mag[:, :, K, :], FN.Sigmoid)
-
-        for i in range(SCALAR_RELU_BLOCKS, BLOCKS):
-            nc.vector.tensor_scalar_max(pos[:, i], t[:, i], 0.0)
-
-        for i in range(BLOCKS):
+            nc.vector.tensor_tensor(t[:, i, K, :], wc[:, i, :], y_sb[:, i, :], ALU.mult)
+            nc.scalar.activation(sgn[:, i], t[:, i], FN.Sign)
             for k in range(TERMS):
                 nc.tensor.matmul(
-                    ps_ramp[i // BANK][:, i % BANK, :],
-                    lhsT=identity[:],
-                    rhs=pos[:, i, k, :],
+                    ps_count[i // PAIR][:, i % PAIR, :],
+                    lhsT=identity_bf[:],
+                    rhs=sgn[:, i, k, :],
                     start=(k == 0),
                     stop=(k == TERMS - 1),
                 )
 
-        prod = held.tile([P, BLOCKS, B], F32, name="prod")
-        lnprod = held.tile([P, BLOCKS, B], F32, name="lnprod")
-        result = held.tile([P, BLOCKS, B], F32, name="result")
-        for g in range(BANKS):
-            group = slice(g * BANK, (g + 1) * BANK)
-            nc.vector.tensor_tensor(prod[:, group, :], sig[:, group, 0, :], sig[:, group, 1, :], ALU.mult)
-            for k in range(2, TERMS):
-                nc.vector.tensor_tensor(prod[:, group, :], prod[:, group, :], sig[:, group, k, :], ALU.mult)
-            nc.scalar.activation(lnprod[:, group, :], prod[:, group, :], FN.Ln)
-            nc.vector.tensor_tensor(result[:, group, :], lnprod[:, group, :], ps_ramp[g][:], ALU.subtract)
-            nc.sync.dma_start(out_blocks[:, group, :], result[:, group, :])
+        def finish(j):
+            pair = slice(j * PAIR, (j + 1) * PAIR)
+            nc.vector.tensor_tensor(loss[:, pair, :], ps_count[j][:], absq[:, pair, :], ALU.mult)
+            nc.vector.scalar_tensor_tensor(
+                out=result[:, pair, :],
+                in0=t[:, pair, K, :],
+                scalar=-TERMS * math.log(2.0),
+                in1=loss[:, pair, :],
+                op0=ALU.add,
+                op1=ALU.subtract,
+            )
+            nc.sync.dma_start(out_blocks[:, pair, :], result[:, pair, :])
+
+        mask(0)
+        look_up(0)
+        for i in range(1, BLOCKS):
+            mask(i)
+
+        ramp = held.tile([P, BLOCKS, B], F32, name="ramp")
+        mag = held.tile([P, BLOCKS, B], F32, name="mag")
+        sig = held.tile([P, BLOCKS, B], F32, name="sig")
+        log2sig = held.tile([P, BLOCKS, B], F32, name="log2sig")
+        ps_q = [psum.tile([P, BANK, B], F32, name=f"ps_q{g}", tag=f"ps_wc{g}") for g in range(BANKS)]
+        nc.vector.tensor_scalar_max(ramp[:], wc[:], 0.0)
+        nc.scalar.activation(mag[:], wc[:], FN.Abs)
+        nc.scalar.activation(sig[:], mag[:], FN.Sigmoid)
+        for g, half in enumerate(halves):
+            nc.tensor.matmul(ps_q[g][:], lhsT=identity[:], rhs=ramp[:, half, :], start=True, stop=False)
+        for g, half in enumerate(halves):
+            nc.scalar.activation(log2sig[:, half, :], sig[:, half, :], FN.Ln, scale=2.0)
+            nc.tensor.matmul(ps_q[g][:], lhsT=minus_identity[:], rhs=log2sig[:, half, :], start=False, stop=True)
+        for g, half in enumerate(halves):
+            nc.scalar.activation(absq[:, half, :], ps_q[g][:], FN.Abs)
+
+        for i in range(1, BLOCKS):
+            look_up(i)
+            if i % PAIR == PAIR - 1 and i // PAIR >= LAG:
+                finish(i // PAIR - LAG)
+        for j in range(PAIRS - LAG, PAIRS):
+            finish(j)

@@ -17,7 +17,6 @@ TERMS = K + 1
 PIECE = B // 16
 BANK = 512 // B
 BANKS = BLOCKS // BANK
-QUAD = 32
 PAIR = 2
 PAIRS = BLOCKS // PAIR
 LAG = 2
@@ -31,59 +30,59 @@ def tile_mf2demo_kernel(tc, codebook, z1, w2, b2, w3, b3, ob, y, offs, out):
         tc.psum_pool(name="psum", bufs=1) as psum,
     ):
         z1_sb = held.tile([H, B], F32, name="z1_sb")
-        nc.sync.dma_start(z1_sb[:], z1)
         w2_sb = held.tile([H, H], BF16, name="w2_sb")
-        nc.sync.dma_start(w2_sb[:], w2)
-        bias_rows = held.tile([P, QUAD], F32, name="bias_rows", align_bytes=64)
-        bias_cols = held.tile([P, QUAD], F32, name="bias_cols", align_bytes=64)
-        nc.vector.memset(bias_rows[:], 0.0)
-        rows_by_quadrant = bias_rows[:].rearrange("(c r) e -> c r e", r=QUAD)
-        nc.sync.dma_start(rows_by_quadrant[:, BLOCKS, :], b2.rearrange("(c e) o -> c (e o)", e=QUAD))
-        b3_by_quadrant = b3.rearrange("(i c e) o -> c i (e o)", i=BLOCKS, e=QUAD)
-        for c in range(P // QUAD):
-            nc.sync.dma_start(bias_rows[c * QUAD : c * QUAD + BLOCKS, :], b3_by_quadrant[c])
-        nc.vector.transpose(bias_cols[:], bias_rows[:])
+        b2_sb = held.tile([H, 1], F32, name="b2_sb")
         w3_sb = held.tile([H, A], BF16, name="w3_sb")
-        nc.sync.dma_start(w3_sb[:], w3)
+        b3_sb = held.tile([P, BLOCKS], F32, name="b3_sb")
         offsets = held.tile([P, N // 16], U16, name="offsets")
-        nc.sync.dma_start(offsets[:], offs)
-
         windows = [held.tile([P, S], F32, name=f"window{i}") for i in range(BLOCKS)]
         ob_sb = held.tile([P, BLOCKS, B], F32, name="ob_sb")
         y_sb = held.tile([P, BLOCKS, B], F32, name="y_sb")
-        ob_blocks = ob.rearrange("(i p) u -> p i u", p=P)
-        y_blocks = y.rearrange("(i p) u -> p i u", p=P)
-        out_blocks = out.rearrange("(i p) u -> p i u", p=P)
+        ob_blocks = ob.rearrange("(p i) u -> p i u", i=BLOCKS)
+        y_blocks = y.rearrange("(p i) u -> p i u", i=BLOCKS)
+        out_blocks = out.rearrange("(p i) u -> p i u", i=BLOCKS)
+        codebook_blocks = codebook.rearrange("(p i) s -> p i s", i=BLOCKS)
+        w3_blocks = w3_sb[:].rearrange("m (p i) -> m i p", i=BLOCKS)
         halves = [slice(first, first + BANK) for first in range(0, BLOCKS, BANK)]
-        nc.sync.dma_start(ob_sb[:, halves[0], :], ob_blocks[:, halves[0], :])
-        nc.sync.dma_start(windows[0][:], codebook[0:P, :])
+        nc.sync.dma_start(z1_sb[:], z1)
+        nc.sync.dma_start(w2_sb[:], w2)
+        nc.sync.dma_start(b2_sb[:], b2)
+        nc.sync.dma_start(w3_sb[:], w3)
+        nc.sync.dma_start(b3_sb[:], b3.rearrange("(p i) o -> p (i o)", i=BLOCKS))
+        nc.sync.dma_start(ob_sb[:, 0:1, :], ob_blocks[:, 0:1, :])
+        nc.sync.dma_start(offsets[:], offs)
+        nc.sync.dma_start(windows[0][:], codebook_blocks[:, 0, :])
+        nc.sync.dma_start(ob_sb[:, 1:BANK, :], ob_blocks[:, 1:BANK, :])
         nc.sync.dma_start(ob_sb[:, halves[1], :], ob_blocks[:, halves[1], :])
+        nc.sync.dma_start(windows[1][:], codebook_blocks[:, 1, :])
         for half in halves:
             nc.sync.dma_start(y_sb[:, half, :], y_blocks[:, half, :])
-            for i in range(max(half.start, 1), half.stop):
-                nc.sync.dma_start(windows[i][:], codebook[i * P : (i + 1) * P, :])
+            for i in range(max(half.start, 2), half.stop):
+                nc.sync.dma_start(windows[i][:], codebook_blocks[:, i, :])
 
         identity = held.tile([P, P], F32, name="identity")
         make_identity(nc, identity[:])
+        half_identity = held.tile([P, P], F32, name="half_identity")
+        nc.gpsimd.tensor_scalar_mul(half_identity[:], identity[:], 0.5)
         minus_identity = held.tile([P, P], F32, name="minus_identity")
-        nc.vector.tensor_scalar_mul(minus_identity[:], identity[:], -1.0)
+        nc.gpsimd.tensor_scalar_mul(minus_identity[:], identity[:], -1.0)
         identity_bf = held.tile([P, P], BF16, name="identity_bf")
-        nc.vector.tensor_copy(identity_bf[:], identity[:])
+        nc.gpsimd.tensor_copy(identity_bf[:], identity[:])
 
         h1 = held.tile([H, B], BF16, name="h1")
         nc.scalar.activation(h1[:], z1_sb[:], FN.Sigmoid)
         ps_h2 = psum.tile([H, B], F32, name="ps_h2")
         nc.tensor.matmul(ps_h2[:], lhsT=w2_sb[:], rhs=h1[:], start=True, stop=True)
         h2 = held.tile([H, B], BF16, name="h2")
-        nc.scalar.activation(h2[:], ps_h2[:], FN.Sigmoid, bias=bias_cols[:, BLOCKS : BLOCKS + 1])
+        nc.scalar.activation(h2[:], ps_h2[:], FN.Sigmoid, bias=b2_sb[:, 0:1])
 
         ps_wc = [psum.tile([P, BANK, B], F32, name=f"ps_wc{g}") for g in range(BANKS)]
         biased = held.tile([P, BLOCKS, B], F32, name="biased")
         wc = held.tile([P, BLOCKS, B], F32, name="wc")
         for i in range(BLOCKS):
             ps_block = ps_wc[i % BANKS][:, i // BANKS, :]
-            nc.tensor.matmul(ps_block, lhsT=w3_sb[:, i * P : (i + 1) * P], rhs=h2[:], start=True, stop=True)
-            nc.scalar.activation(biased[:, i, :], ps_block, FN.Identity, bias=bias_cols[:, i : i + 1])
+            nc.tensor.matmul(ps_block, lhsT=w3_blocks[:, i, :], rhs=h2[:], start=True, stop=True)
+            nc.scalar.activation(biased[:, i, :], ps_block, FN.Identity, bias=b3_sb[:, i : i + 1])
 
         t = held.tile([P, BLOCKS, TERMS, B], F32, name="t")
         sgn = held.tile([P, BLOCKS, TERMS, B], BF16, name="sgn")
@@ -132,16 +131,15 @@ def tile_mf2demo_kernel(tc, codebook, z1, w2, b2, w3, b3, ob, y, offs, out):
         for i in range(1, BLOCKS):
             mask(i)
 
-        ramp = held.tile([P, BLOCKS, B], F32, name="ramp")
         mag = held.tile([P, BLOCKS, B], F32, name="mag")
         sig = held.tile([P, BLOCKS, B], F32, name="sig")
         log2sig = held.tile([P, BLOCKS, B], F32, name="log2sig")
         ps_q = [psum.tile([P, BANK, B], F32, name=f"ps_q{g}", tag=f"ps_wc{g}") for g in range(BANKS)]
-        nc.vector.tensor_scalar_max(ramp[:], wc[:], 0.0)
         nc.scalar.activation(mag[:], wc[:], FN.Abs)
         nc.scalar.activation(sig[:], mag[:], FN.Sigmoid)
         for g, half in enumerate(halves):
-            nc.tensor.matmul(ps_q[g][:], lhsT=identity[:], rhs=ramp[:, half, :], start=True, stop=False)
+            nc.tensor.matmul(ps_q[g][:], lhsT=half_identity[:], rhs=wc[:, half, :], start=True, stop=False)
+            nc.tensor.matmul(ps_q[g][:], lhsT=half_identity[:], rhs=mag[:, half, :], start=False, stop=False)
         for g, half in enumerate(halves):
             nc.scalar.activation(log2sig[:, half, :], sig[:, half, :], FN.Ln, scale=2.0)
             nc.tensor.matmul(ps_q[g][:], lhsT=minus_identity[:], rhs=log2sig[:, half, :], start=False, stop=True)

@@ -113,18 +113,18 @@ def tile_mf2demo_kernel(tc, codebook, z1, w2, b2, w3, b3, ob, y, offs, out):
                     stop=(k == TERMS - 1),
                 )
 
-        def finish(j):
-            pair = slice(j * PAIR, (j + 1) * PAIR)
-            nc.vector.tensor_tensor(loss[:, pair, :], ps_count[j][:], absq[:, pair, :], ALU.mult)
+        def finish(blocks):
+            count = ps_count[blocks.start // PAIR][:, blocks.start % PAIR : blocks.start % PAIR + blocks.stop - blocks.start, :]
+            nc.vector.tensor_tensor(loss[:, blocks, :], count, absq[:, blocks, :], ALU.mult)
             nc.vector.scalar_tensor_tensor(
-                out=result[:, pair, :],
-                in0=t[:, pair, K, :],
+                out=result[:, blocks, :],
+                in0=t[:, blocks, K, :],
                 scalar=-TERMS * math.log(2.0),
-                in1=loss[:, pair, :],
+                in1=loss[:, blocks, :],
                 op0=ALU.add,
                 op1=ALU.subtract,
             )
-            nc.sync.dma_start(out_blocks[:, pair, :], result[:, pair, :])
+            nc.sync.dma_start(out_blocks[:, blocks, :], result[:, blocks, :])
 
         mask(0)
         look_up(0)
@@ -149,6 +149,8 @@ def tile_mf2demo_kernel(tc, codebook, z1, w2, b2, w3, b3, ob, y, offs, out):
         for i in range(1, BLOCKS):
             look_up(i)
             if i % PAIR == PAIR - 1 and i // PAIR >= LAG:
-                finish(i // PAIR - LAG)
-        for j in range(PAIRS - LAG, PAIRS):
-            finish(j)
+                finish(slice(i + 1 - (LAG + 1) * PAIR, i + 1 - LAG * PAIR))
+        for first in range(BLOCKS - LAG * PAIR, BLOCKS - PAIR, PAIR):
+            finish(slice(first, first + PAIR))
+        for i in range(BLOCKS - PAIR, BLOCKS):
+            finish(slice(i, i + 1))

@@ -17,9 +17,6 @@ TERMS = K + 1
 PIECE = B // 16
 BANK = 512 // B
 BANKS = BLOCKS // BANK
-PAIR = 2
-PAIRS = BLOCKS // PAIR
-LAG = 2
 
 FLOPS = 2 * H * H * B + 2 * H * A * B
 
@@ -62,8 +59,6 @@ def tile_mf2demo_kernel(tc, codebook, z1, w2, b2, w3, b3, ob, y, offs, out):
 
         identity = held.tile([P, P], F32, name="identity")
         make_identity(nc, identity[:])
-        half_identity = held.tile([P, P], F32, name="half_identity")
-        nc.gpsimd.tensor_scalar_mul(half_identity[:], identity[:], 0.5)
         minus_identity = held.tile([P, P], F32, name="minus_identity")
         nc.gpsimd.tensor_scalar_mul(minus_identity[:], identity[:], -1.0)
         identity_bf = held.tile([P, P], BF16, name="identity_bf")
@@ -76,81 +71,94 @@ def tile_mf2demo_kernel(tc, codebook, z1, w2, b2, w3, b3, ob, y, offs, out):
         h2 = held.tile([H, B], BF16, name="h2")
         nc.scalar.activation(h2[:], ps_h2[:], FN.Sigmoid, bias=b2_sb[:, 0:1])
 
-        ps_wc = [psum.tile([P, BANK, B], F32, name=f"ps_wc{g}") for g in range(BANKS)]
-        biased = held.tile([P, BLOCKS, B], F32, name="biased")
-        wc = held.tile([P, BLOCKS, B], F32, name="wc")
-        for i in range(BLOCKS):
-            ps_block = ps_wc[i % BANKS][:, i // BANKS, :]
-            nc.tensor.matmul(ps_block, lhsT=w3_blocks[:, i, :], rhs=h2[:], start=True, stop=True)
-            nc.scalar.activation(biased[:, i, :], ps_block, FN.Identity, bias=b3_sb[:, i : i + 1])
+        x_groups = [slice(0, 1), slice(1, BANK), slice(BANK, BLOCKS)]
+        x = [None] * BLOCKS
+        for g, group in enumerate(x_groups):
+            ps_x = psum.tile([P, BANK, B], F32, name=f"ps_x{g}")
+            for i in range(group.start, group.stop):
+                x[i] = ps_x[:, i - group.start, :]
+                nc.tensor.matmul(x[i], lhsT=w3_blocks[:, i, :], rhs=h2[:], start=True, stop=True)
 
+        wc_twice = held.tile([P, BLOCKS, 2, B], F32, name="wc_twice")
+        wc = wc_twice[:, :, 0, :]
         t = held.tile([P, BLOCKS, TERMS, B], F32, name="t")
         sgn = held.tile([P, BLOCKS, TERMS, B], BF16, name="sgn")
-        ps_count = [psum.tile([P, PAIR, B], F32, name=f"ps_count{j}") for j in range(PAIRS)]
-        absq = held.tile([P, BLOCKS, B], F32, name="absq")
-        loss = held.tile([P, BLOCKS, B], F32, name="loss")
-        result = held.tile([P, BLOCKS, B], F32, name="result")
 
         def mask(i):
-            nc.vector.tensor_tensor(wc[:, i, :], biased[:, i, :], ob_sb[:, i, :], ALU.mult)
+            nc.vector.scalar_tensor_tensor(
+                out=wc[:, i, :], in0=x[i], scalar=b3_sb[:, i : i + 1], in1=ob_sb[:, i, :], op0=ALU.add, op1=ALU.mult
+            )
 
-        def look_up(i):
-            for k in range(K):
+        def positive(i):
+            nc.vector.tensor_tensor(t[:, i, 0, :], wc[:, i, :], y_sb[:, i, :], ALU.mult)
+
+        def look_up(i, at_once):
+            for k in range(0, K, at_once):
                 nc.vector.tensor_tensor(
-                    t[:, i, k, :],
-                    windows[i][:].indirect(offsets[:, k * PIECE : (k + 1) * PIECE]),
-                    wc[:, i, :],
+                    t[:, i, 1 + k : 1 + k + at_once, :].rearrange("p k u -> p (k u)"),
+                    windows[i][:].indirect(offsets[:, k * PIECE : (k + at_once) * PIECE]),
+                    wc_twice[:, i, 0:at_once, :].rearrange("p k u -> p (k u)"),
                     ALU.mult,
                 )
-            nc.vector.tensor_tensor(t[:, i, K, :], wc[:, i, :], y_sb[:, i, :], ALU.mult)
-            nc.scalar.activation(sgn[:, i], t[:, i], FN.Sign)
-            for k in range(TERMS):
-                nc.tensor.matmul(
-                    ps_count[i // PAIR][:, i % PAIR, :],
-                    lhsT=identity_bf[:],
-                    rhs=sgn[:, i, k, :],
-                    start=(k == 0),
-                    stop=(k == TERMS - 1),
-                )
-
-        def finish(blocks):
-            count = ps_count[blocks.start // PAIR][:, blocks.start % PAIR : blocks.start % PAIR + blocks.stop - blocks.start, :]
-            nc.vector.tensor_tensor(loss[:, blocks, :], count, absq[:, blocks, :], ALU.mult)
-            nc.vector.scalar_tensor_tensor(
-                out=result[:, blocks, :],
-                in0=t[:, blocks, K, :],
-                scalar=-TERMS * math.log(2.0),
-                in1=loss[:, blocks, :],
-                op0=ALU.add,
-                op1=ALU.subtract,
-            )
-            nc.sync.dma_start(out_blocks[:, blocks, :], result[:, blocks, :])
-
-        mask(0)
-        look_up(0)
-        for i in range(1, BLOCKS):
-            mask(i)
 
         mag = held.tile([P, BLOCKS, B], F32, name="mag")
+        ramp = held.tile([P, BLOCKS, B], F32, name="ramp")
+        mask(0)
+        for i in range(BLOCKS):
+            nc.scalar.activation(mag[:, i, :], x[i], FN.Abs, bias=b3_sb[:, i : i + 1])
+        look_up(0, at_once=1)
+        for i in range(1, BLOCKS):
+            mask(i)
+        look_up(1, at_once=1)
+        nc.vector.tensor_copy(wc_twice[:, 2:, 1, :], wc[:, 2:, :])
+        positive(0)
+        positive(1)
+
         sig = held.tile([P, BLOCKS, B], F32, name="sig")
         log2sig = held.tile([P, BLOCKS, B], F32, name="log2sig")
-        ps_q = [psum.tile([P, BANK, B], F32, name=f"ps_q{g}", tag=f"ps_wc{g}") for g in range(BANKS)]
-        nc.scalar.activation(mag[:], wc[:], FN.Abs)
+        absq = held.tile([P, BLOCKS, B], F32, name="absq")
+        ps_q = [psum.tile([P, BANK, B], F32, name=f"ps_q{g}") for g in range(BANKS)]
         nc.scalar.activation(sig[:], mag[:], FN.Sigmoid)
+        for i in range(BLOCKS):
+            nc.scalar.activation(ramp[:, i, :], x[i], FN.Relu, bias=b3_sb[:, i : i + 1])
         for g, half in enumerate(halves):
-            nc.tensor.matmul(ps_q[g][:], lhsT=half_identity[:], rhs=wc[:, half, :], start=True, stop=False)
-            nc.tensor.matmul(ps_q[g][:], lhsT=half_identity[:], rhs=mag[:, half, :], start=False, stop=False)
+            nc.tensor.matmul(ps_q[g][:], lhsT=identity[:], rhs=ramp[:, half, :], start=True, stop=False)
         for g, half in enumerate(halves):
             nc.scalar.activation(log2sig[:, half, :], sig[:, half, :], FN.Ln, scale=2.0)
             nc.tensor.matmul(ps_q[g][:], lhsT=minus_identity[:], rhs=log2sig[:, half, :], start=False, stop=True)
         for g, half in enumerate(halves):
             nc.scalar.activation(absq[:, half, :], ps_q[g][:], FN.Abs)
 
-        for i in range(1, BLOCKS):
-            look_up(i)
-            if i % PAIR == PAIR - 1 and i // PAIR >= LAG:
-                finish(slice(i + 1 - (LAG + 1) * PAIR, i + 1 - LAG * PAIR))
-        for first in range(BLOCKS - LAG * PAIR, BLOCKS - PAIR, PAIR):
-            finish(slice(first, first + PAIR))
-        for i in range(BLOCKS - PAIR, BLOCKS):
-            finish(slice(i, i + 1))
+        loss = held.tile([P, BLOCKS, B], F32, name="loss")
+        result = held.tile([P, BLOCKS, B], F32, name="result")
+        groups = [slice(0, 4), slice(4, 6), slice(6, 7), slice(7, 8)]
+        bank_tags = ["ps_x1", "ps_x2", "ps_last", "ps_x0"]
+        counts = [psum.tile([P, BANK, B], F32, name=f"ps_count{g}", tag=tag) for g, tag in enumerate(bank_tags)]
+
+        def count_signs(count, i, parts):
+            for part in parts:
+                nc.scalar.activation(sgn[:, i, part, :], t[:, i, part, :], FN.Sign)
+            for k in range(TERMS):
+                nc.tensor.matmul(
+                    count, lhsT=identity_bf[:], rhs=sgn[:, i, k, :], start=(k == 0), stop=(k == TERMS - 1)
+                )
+
+        for group, ps_count in zip(groups, counts):
+            for i in range(group.start, group.stop):
+                if i >= 2:
+                    positive(i)
+                    look_up(i, at_once=2)
+                parts = [slice(0, 3), slice(3, TERMS)] if i == BLOCKS - 1 else [slice(0, TERMS)]
+                count_signs(ps_count[:, i - group.start, :], i, parts)
+        for group, ps_count in zip(groups, counts):
+            count = ps_count[:, 0 : group.stop - group.start, :]
+            nc.vector.tensor_tensor(loss[:, group, :], count, absq[:, group, :], ALU.mult)
+            nc.vector.scalar_tensor_tensor(
+                out=result[:, group, :],
+                in0=t[:, group, 0, :],
+                scalar=-TERMS * math.log(2.0),
+                in1=loss[:, group, :],
+                op0=ALU.add,
+                op1=ALU.subtract,
+            )
+            nc.sync.dma_start(out_blocks[:, group, :], result[:, group, :])

@@ -17,6 +17,7 @@ TERMS = K + 1
 PIECE = B // 16
 BANK = 512 // B
 BANKS = BLOCKS // BANK
+SINGLE = 3
 
 FLOPS = 2 * H * H * B + 2 * H * A * B
 
@@ -89,8 +90,8 @@ def tile_mf2demo_kernel(tc, codebook, z1, w2, b2, w3, b3, ob, y, offs, out):
                 out=wc[:, i, :], in0=x[i], scalar=b3_sb[:, i : i + 1], in1=ob_sb[:, i, :], op0=ALU.add, op1=ALU.mult
             )
 
-        def positive(i):
-            nc.vector.tensor_tensor(t[:, i, 0, :], wc[:, i, :], y_sb[:, i, :], ALU.mult)
+        def positive(blocks):
+            nc.vector.tensor_tensor(t[:, blocks, 0, :], wc[:, blocks, :], y_sb[:, blocks, :], ALU.mult)
 
         def look_up(i, at_once):
             for k in range(0, K, at_once):
@@ -103,36 +104,42 @@ def tile_mf2demo_kernel(tc, codebook, z1, w2, b2, w3, b3, ob, y, offs, out):
 
         mag = held.tile([P, BLOCKS, B], F32, name="mag")
         ramp = held.tile([P, BLOCKS, B], F32, name="ramp")
+
+        def take_ramp(i):
+            nc.scalar.activation(ramp[:, i, :], x[i], FN.Relu, bias=b3_sb[:, i : i + 1])
+
         mask(0)
         for i in range(BLOCKS):
             nc.scalar.activation(mag[:, i, :], x[i], FN.Abs, bias=b3_sb[:, i : i + 1])
+        for i in range(BANK, BLOCKS):
+            take_ramp(i)
         look_up(0, at_once=1)
         for i in range(1, BLOCKS):
             mask(i)
+        nc.sync.dma_start(wc_twice[:, SINGLE:, 1, :], wc[:, SINGLE:, :])
         look_up(1, at_once=1)
-        nc.vector.tensor_copy(wc_twice[:, 2:, 1, :], wc[:, 2:, :])
-        positive(0)
-        positive(1)
+        positive(slice(0, 2))
 
         sig = held.tile([P, BLOCKS, B], F32, name="sig")
         log2sig = held.tile([P, BLOCKS, B], F32, name="log2sig")
         absq = held.tile([P, BLOCKS, B], F32, name="absq")
         ps_q = [psum.tile([P, BANK, B], F32, name=f"ps_q{g}") for g in range(BANKS)]
         nc.scalar.activation(sig[:], mag[:], FN.Sigmoid)
-        for i in range(BLOCKS):
-            nc.scalar.activation(ramp[:, i, :], x[i], FN.Relu, bias=b3_sb[:, i : i + 1])
+        for i in range(BANK):
+            take_ramp(i)
         for g, half in enumerate(halves):
             nc.tensor.matmul(ps_q[g][:], lhsT=identity[:], rhs=ramp[:, half, :], start=True, stop=False)
         for g, half in enumerate(halves):
             nc.scalar.activation(log2sig[:, half, :], sig[:, half, :], FN.Ln, scale=2.0)
             nc.tensor.matmul(ps_q[g][:], lhsT=minus_identity[:], rhs=log2sig[:, half, :], start=False, stop=True)
-        for g, half in enumerate(halves):
-            nc.scalar.activation(absq[:, half, :], ps_q[g][:], FN.Abs)
+
+        def take_absq(g):
+            nc.scalar.activation(absq[:, halves[g], :], ps_q[g][:], FN.Abs)
 
         loss = held.tile([P, BLOCKS, B], F32, name="loss")
         result = held.tile([P, BLOCKS, B], F32, name="result")
-        groups = [slice(0, 4), slice(4, 6), slice(6, 7), slice(7, 8)]
-        bank_tags = ["ps_x1", "ps_x2", "ps_last", "ps_x0"]
+        groups = [slice(0, 4), slice(4, 6), slice(6, 8)]
+        bank_tags = ["ps_x1", "ps_x2", "ps_x0"]
         counts = [psum.tile([P, BANK, B], F32, name=f"ps_count{g}", tag=tag) for g, tag in enumerate(bank_tags)]
 
         def count_signs(count, i, parts):
@@ -146,19 +153,26 @@ def tile_mf2demo_kernel(tc, codebook, z1, w2, b2, w3, b3, ob, y, offs, out):
         for group, ps_count in zip(groups, counts):
             for i in range(group.start, group.stop):
                 if i >= 2:
-                    positive(i)
-                    look_up(i, at_once=2)
+                    if i % 2 == 0:
+                        positive(slice(i, i + 2))
+                    look_up(i, at_once=1 if i < SINGLE else 2)
                 parts = [slice(0, 3), slice(3, TERMS)] if i == BLOCKS - 1 else [slice(0, TERMS)]
                 count_signs(ps_count[:, i - group.start, :], i, parts)
+                if i in (2, 6):
+                    take_absq(i // BANK)
         for group, ps_count in zip(groups, counts):
-            count = ps_count[:, 0 : group.stop - group.start, :]
-            nc.vector.tensor_tensor(loss[:, group, :], count, absq[:, group, :], ALU.mult)
-            nc.vector.scalar_tensor_tensor(
-                out=result[:, group, :],
-                in0=t[:, group, 0, :],
-                scalar=-TERMS * math.log(2.0),
-                in1=loss[:, group, :],
-                op0=ALU.add,
-                op1=ALU.subtract,
-            )
-            nc.sync.dma_start(out_blocks[:, group, :], result[:, group, :])
+            half = (group.stop - group.start) // 2
+            parts = [slice(first, first + half) for first in range(group.start, group.stop, half)]
+            for part in parts:
+                count = ps_count[:, part.start - group.start : part.stop - group.start, :]
+                nc.vector.tensor_tensor(loss[:, part, :], count, absq[:, part, :], ALU.mult)
+            for part in parts:
+                nc.vector.scalar_tensor_tensor(
+                    out=result[:, part, :],
+                    in0=t[:, part, 0, :],
+                    scalar=-TERMS * math.log(2.0),
+                    in1=loss[:, part, :],
+                    op0=ALU.add,
+                    op1=ALU.subtract,
+                )
+                nc.sync.dma_start(out_blocks[:, part, :], result[:, part, :])

@@ -17,7 +17,7 @@ TERMS = K + 1
 PIECE = B // 16
 BANK = 512 // B
 BANKS = BLOCKS // BANK
-SINGLE = 3
+SINGLE = 2
 
 FLOPS = 2 * H * H * B + 2 * H * A * B
 
@@ -114,11 +114,13 @@ def tile_mf2demo_kernel(tc, codebook, z1, w2, b2, w3, b3, ob, y, offs, out):
         for i in range(BANK, BLOCKS):
             take_ramp(i)
         look_up(0, at_once=1)
-        for i in range(1, BLOCKS):
-            mask(i)
-        nc.sync.dma_start(wc_twice[:, SINGLE:, 1, :], wc[:, SINGLE:, :])
+        for group in (slice(1, BANK), slice(BANK, BLOCKS)):
+            for i in range(group.start, group.stop):
+                mask(i)
+            copied = slice(max(group.start, SINGLE), group.stop)
+            nc.sync.dma_start(wc_twice[:, copied, 1, :], wc[:, copied, :])
         look_up(1, at_once=1)
-        positive(slice(0, 2))
+        positive(halves[0])
 
         sig = held.tile([P, BLOCKS, B], F32, name="sig")
         log2sig = held.tile([P, BLOCKS, B], F32, name="log2sig")
@@ -153,8 +155,8 @@ def tile_mf2demo_kernel(tc, codebook, z1, w2, b2, w3, b3, ob, y, offs, out):
         for group, ps_count in zip(groups, counts):
             for i in range(group.start, group.stop):
                 if i >= 2:
-                    if i % 2 == 0:
-                        positive(slice(i, i + 2))
+                    if i == BANK:
+                        positive(halves[1])
                     look_up(i, at_once=1 if i < SINGLE else 2)
                 parts = [slice(0, 3), slice(3, TERMS)] if i == BLOCKS - 1 else [slice(0, TERMS)]
                 count_signs(ps_count[:, i - group.start, :], i, parts)

@@ -17,7 +17,7 @@ TERMS = K + 1
 PIECE = B // 16
 BANK = 512 // B
 BANKS = BLOCKS // BANK
-SINGLE = 2
+SINGLE = 3
 
 FLOPS = 2 * H * H * B + 2 * H * A * B
 
@@ -114,13 +114,13 @@ def tile_mf2demo_kernel(tc, codebook, z1, w2, b2, w3, b3, ob, y, offs, out):
         for i in range(BANK, BLOCKS):
             take_ramp(i)
         look_up(0, at_once=1)
-        for group in (slice(1, BANK), slice(BANK, BLOCKS)):
-            for i in range(group.start, group.stop):
-                mask(i)
-            copied = slice(max(group.start, SINGLE), group.stop)
-            nc.sync.dma_start(wc_twice[:, copied, 1, :], wc[:, copied, :])
-        look_up(1, at_once=1)
-        positive(halves[0])
+        for i in range(1, BLOCKS):
+            mask(i)
+        nc.sync.dma_start(wc_twice[:, SINGLE:, 1, :], wc[:, SINGLE:, :])
+        for i in range(1, SINGLE):
+            look_up(i, at_once=1)
+        for half in halves:
+            positive(half)
 
         sig = held.tile([P, BLOCKS, B], F32, name="sig")
         log2sig = held.tile([P, BLOCKS, B], F32, name="log2sig")
@@ -140,8 +140,8 @@ def tile_mf2demo_kernel(tc, codebook, z1, w2, b2, w3, b3, ob, y, offs, out):
 
         loss = held.tile([P, BLOCKS, B], F32, name="loss")
         result = held.tile([P, BLOCKS, B], F32, name="result")
-        groups = [slice(0, 4), slice(4, 6), slice(6, 8)]
-        bank_tags = ["ps_x1", "ps_x2", "ps_x0"]
+        groups = halves
+        bank_tags = ["ps_x1", "ps_x2"]
         counts = [psum.tile([P, BANK, B], F32, name=f"ps_count{g}", tag=tag) for g, tag in enumerate(bank_tags)]
 
         def count_signs(count, i, parts):
@@ -154,17 +154,15 @@ def tile_mf2demo_kernel(tc, codebook, z1, w2, b2, w3, b3, ob, y, offs, out):
 
         for group, ps_count in zip(groups, counts):
             for i in range(group.start, group.stop):
-                if i >= 2:
-                    if i == BANK:
-                        positive(halves[1])
-                    look_up(i, at_once=1 if i < SINGLE else 2)
+                if i >= SINGLE:
+                    look_up(i, at_once=2)
                 parts = [slice(0, 3), slice(3, TERMS)] if i == BLOCKS - 1 else [slice(0, TERMS)]
                 count_signs(ps_count[:, i - group.start, :], i, parts)
                 if i in (2, 6):
                     take_absq(i // BANK)
         for group, ps_count in zip(groups, counts):
-            half = (group.stop - group.start) // 2
-            parts = [slice(first, first + half) for first in range(group.start, group.stop, half)]
+            middle = group.start + BANK // 2 if group.stop < BLOCKS else BLOCKS - 1
+            parts = [slice(group.start, middle), slice(middle, group.stop)]
             for part in parts:
                 count = ps_count[:, part.start - group.start : part.stop - group.start, :]
                 nc.vector.tensor_tensor(loss[:, part, :], count, absq[:, part, :], ALU.mult)

@@ -140,8 +140,8 @@ def tile_mf2demo_kernel(tc, codebook, z1, w2, b2, w3, b3, ob, y, offs, out):
 
         loss = held.tile([P, BLOCKS, B], F32, name="loss")
         result = held.tile([P, BLOCKS, B], F32, name="result")
-        groups = halves
-        bank_tags = ["ps_x1", "ps_x2"]
+        groups = [slice(0, 4), slice(4, 6), slice(6, 8)]
+        bank_tags = ["ps_x1", "ps_x2", "ps_x0"]
         counts = [psum.tile([P, BANK, B], F32, name=f"ps_count{g}", tag=tag) for g, tag in enumerate(bank_tags)]
 
         def count_signs(count, i, parts):
@@ -161,8 +161,8 @@ def tile_mf2demo_kernel(tc, codebook, z1, w2, b2, w3, b3, ob, y, offs, out):
                 if i in (2, 6):
                     take_absq(i // BANK)
         for group, ps_count in zip(groups, counts):
-            middle = group.start + BANK // 2 if group.stop < BLOCKS else BLOCKS - 1
-            parts = [slice(group.start, middle), slice(middle, group.stop)]
+            half = (group.stop - group.start) // 2
+            parts = [slice(first, first + half) for first in range(group.start, group.stop, half)]
             for part in parts:
                 count = ps_count[:, part.start - group.start : part.stop - group.start, :]
                 nc.vector.tensor_tensor(loss[:, part, :], count, absq[:, part, :], ALU.mult)

import math

import concourse.mybir as mybir
from concourse.masks import make_identity

F32 = mybir.dt.float32
BF16 = mybir.dt.bfloat16
U16 = mybir.dt.uint16
ALU = mybir.AluOpType
FN = mybir.ActivationFunctionType

P = 128
A, S, B, K, H = 1024, 256, 128, 4, 128
N = K * B
BLOCKS = A // P
TERMS = K + 1
PIECE = B // 16
BANK = 512 // B
BANKS = BLOCKS // BANK
SINGLE = 3

FLOPS = 2 * H * H * B + 2 * H * A * B

def tile_mf2demo_kernel(tc, codebook, z1, w2, b2, w3, b3, ob, y, offs, out):
    nc = tc.nc
    with (
        tc.tile_pool(name="held", bufs=1) as held,
        tc.psum_pool(name="psum", bufs=1) as psum,
    ):
        z1_sb = held.tile([H, B], F32, name="z1_sb")
        w2_sb = held.tile([H, H], BF16, name="w2_sb")
        b2_sb = held.tile([H, 1], F32, name="b2_sb")
        w3_sb = held.tile([H, A], BF16, name="w3_sb")
        b3_sb = held.tile([P, BLOCKS], F32, name="b3_sb")
        offsets = held.tile([P, N // 16], U16, name="offsets")
        windows = [held.tile([P, S], F32, name=f"window{i}") for i in range(BLOCKS)]
        ob_sb = held.tile([P, BLOCKS, B], F32, name="ob_sb")
        y_sb = held.tile([P, BLOCKS, B], F32, name="y_sb")
        ob_blocks = ob.rearrange("(p i) u -> p i u", i=BLOCKS)
        y_blocks = y.rearrange("(p i) u -> p i u", i=BLOCKS)
        out_blocks = out.rearrange("(p i) u -> p i u", i=BLOCKS)
        codebook_blocks = codebook.rearrange("(p i) s -> p i s", i=BLOCKS)
        w3_blocks = w3_sb[:].rearrange("m (p i) -> m i p", i=BLOCKS)
        halves = [slice(first, first + BANK) for first in range(0, BLOCKS, BANK)]
        nc.sync.dma_start(z1_sb[:], z1)
        nc.sync.dma_start(w2_sb[:], w2)
        nc.sync.dma_start(b2_sb[:], b2)
        nc.sync.dma_start(w3_sb[:], w3)
        nc.sync.dma_start(b3_sb[:], b3.rearrange("(p i) o -> p (i o)", i=BLOCKS))
        nc.sync.dma_start(ob_sb[:, 0:1, :], ob_blocks[:, 0:1, :])
        nc.sync.dma_start(offsets[:], offs)
        nc.sync.dma_start(windows[0][:], codebook_blocks[:, 0, :])
        nc.sync.dma_start(ob_sb[:, 1:BANK, :], ob_blocks[:, 1:BANK, :])
        nc.sync.dma_start(ob_sb[:, halves[1], :], ob_blocks[:, halves[1], :])
        nc.sync.dma_start(windows[1][:], codebook_blocks[:, 1, :])
        for half in halves:
            nc.sync.dma_start(y_sb[:, half, :], y_blocks[:, half, :])
            for i in range(max(half.start, 2), half.stop):
                nc.sync.dma_start(windows[i][:], codebook_blocks[:, i, :])

        identity = held.tile([P, P], F32, name="identity")
        make_identity(nc, identity[:])
        minus_identity = held.tile([P, P], F32, name="minus_identity")
        nc.gpsimd.tensor_scalar_mul(minus_identity[:], identity[:], -1.0)
        identity_bf = held.tile([P, P], BF16, name="identity_bf")
        nc.gpsimd.tensor_copy(identity_bf[:], identity[:])

        h1 = held.tile([H, B], BF16, name="h1")
        nc.scalar.activation(h1[:], z1_sb[:], FN.Sigmoid)
        ps_h2 = psum.tile([H, B], F32, name="ps_h2")
        nc.tensor.matmul(ps_h2[:], lhsT=w2_sb[:], rhs=h1[:], start=True, stop=True)
        h2 = held.tile([H, B], BF16, name="h2")
        nc.scalar.activation(h2[:], ps_h2[:], FN.Sigmoid, bias=b2_sb[:, 0:1])

        x_groups = [slice(0, 1), slice(1, BANK), slice(BANK, BLOCKS)]
        x = [None] * BLOCKS
        for g, group in enumerate(x_groups):
            ps_x = psum.tile([P, BANK, B], F32, name=f"ps_x{g}")
            for i in range(group.start, group.stop):
                x[i] = ps_x[:, i - group.start, :]
                nc.tensor.matmul(x[i], lhsT=w3_blocks[:, i, :], rhs=h2[:], start=True, stop=True)

        wc_twice = held.tile([P, BLOCKS, 2, B], F32, name="wc_twice")
        wc = wc_twice[:, :, 0, :]
        t = held.tile([P, BLOCKS, TERMS, B], F32, name="t")
        sgn = held.tile([P, BLOCKS, TERMS, B], BF16, name="sgn")

        def mask(i):
            nc.vector.scalar_tensor_tensor(
                out=wc[:, i, :], in0=x[i], scalar=b3_sb[:, i : i + 1], in1=ob_sb[:, i, :], op0=ALU.add, op1=ALU.mult
            )

        def positive(blocks):
            nc.vector.tensor_tensor(t[:, blocks, 0, :], wc[:, blocks, :], y_sb[:, blocks, :], ALU.mult)

        def look_up(i, at_once):
            for k in range(0, K, at_once):
                nc.vector.tensor_tensor(
                    t[:, i, 1 + k : 1 + k + at_once, :].rearrange("p k u -> p (k u)"),
                    windows[i][:].indirect(offsets[:, k * PIECE : (k + at_once) * PIECE]),
                    wc_twice[:, i, 0:at_once, :].rearrange("p k u -> p (k u)"),
                    ALU.mult,
                )

        mag = held.tile([P, BLOCKS, B], F32, name="mag")
        ramp = held.tile([P, BLOCKS, B], F32, name="ramp")

        def take_ramp(i):
            nc.scalar.activation(ramp[:, i, :], x[i], FN.Relu, bias=b3_sb[:, i : i + 1])

        mask(0)
        for i in range(BLOCKS):
            nc.scalar.activation(mag[:, i, :], x[i], FN.Abs, bias=b3_sb[:, i : i + 1])
        for i in range(BANK, BLOCKS):
            take_ramp(i)
        look_up(0, at_once=1)
        for i in range(1, BLOCKS):
            mask(i)
        nc.sync.dma_start(wc_twice[:, SINGLE:, 1, :], wc[:, SINGLE:, :])
        for i in range(1, SINGLE):
            look_up(i, at_once=1)
        for half in halves:
            positive(half)

        sig = held.tile([P, BLOCKS, B], F32, name="sig")
        log2sig = held.tile([P, BLOCKS, B], F32, name="log2sig")
        absq = held.tile([P, BLOCKS, B], F32, name="absq")
        ps_q = [psum.tile([P, BANK, B], F32, name=f"ps_q{g}") for g in range(BANKS)]
        nc.scalar.activation(sig[:], mag[:], FN.Sigmoid)
        for i in range(BANK):
            take_ramp(i)
        for g, half in enumerate(halves):
            nc.tensor.matmul(ps_q[g][:], lhsT=identity[:], rhs=ramp[:, half, :], start=True, stop=False)
        for g, half in enumerate(halves):
            nc.scalar.activation(log2sig[:, half, :], sig[:, half, :], FN.Ln, scale=2.0)
            nc.tensor.matmul(ps_q[g][:], lhsT=minus_identity[:], rhs=log2sig[:, half, :], start=False, stop=True)

        def take_absq(g):
            nc.scalar.activation(absq[:, halves[g], :], ps_q[g][:], FN.Abs)

        loss = held.tile([P, BLOCKS, B], F32, name="loss")
        result = held.tile([P, BLOCKS, B], F32, name="result")
        groups = [slice(0, 4), slice(4, 6), slice(6, 8)]
        bank_tags = ["ps_x1", "ps_x2", "ps_x0"]
        counts = [psum.tile([P, BANK, B], F32, name=f"ps_count{g}", tag=tag) for g, tag in enumerate(bank_tags)]

        def count_signs(count, i, parts):
            for part in parts:
                nc.scalar.activation(sgn[:, i, part, :], t[:, i, part, :], FN.Sign)
            for k in range(TERMS):
                nc.tensor.matmul(
                    count, lhsT=identity_bf[:], rhs=sgn[:, i, k, :], start=(k == 0), stop=(k == TERMS - 1)
                )

        for group, ps_count in zip(groups, counts):
            for i in range(group.start, group.stop):
                if i >= SINGLE:
                    look_up(i, at_once=2)
                parts = [slice(0, 3), slice(3, TERMS)] if i == BLOCKS - 1 else [slice(0, TERMS)]
                count_signs(ps_count[:, i - group.start, :], i, parts)
                if i in (2, 6):
                    take_absq(i // BANK)
        for group, ps_count in zip(groups, counts):
            half = (group.stop - group.start) // 2
            parts = [slice(first, first + half) for first in range(group.start, group.stop, half)]
            for part in parts:
                count = ps_count[:, part.start - group.start : part.stop - group.start, :]
                nc.vector.tensor_tensor(loss[:, part, :], count, absq[:, part, :], ALU.mult)
            for part in parts:
                nc.vector.scalar_tensor_tensor(
                    out=result[:, part, :],
                    in0=t[:, part, 0, :],
                    scalar=-TERMS * math.log(2.0),
                    in1=loss[:, part, :],
                    op0=ALU.add,
                    op1=ALU.subtract,
                )
                nc.sync.dma_start(out_blocks[:, part, :], result[:, part, :])
